import numpy as np
import ml_dtypes

BF16 = ml_dtypes.bfloat16


def bf(x):
    return np.asarray(x, np.float32).astype(BF16)


def f32(x):
    return np.asarray(x, np.float32)


def f64(x):
    return np.asarray(x).astype(np.float64)


def striped(idx):
    return np.tile(idx.reshape(-1, 16).T, (8, 1))


C, S, N, D = 384, 4096, 1024, 256


def into_ball(v, scale):
    n = np.linalg.norm(v, axis=0, keepdims=True)
    return v * (scale / (1.0 + n))


def setup_inputs():
    base = f32(np.random.uniform(0.5, 10.0, (C, S)))
    pts = bf(into_ball(np.random.standard_normal((D, C)), np.random.uniform(0.3, 0.8, (1, C))))
    cent = bf(into_ball(np.random.standard_normal((D, N)), np.random.uniform(0.3, 0.8, (1, N))))
    return {"base": base, "pts": pts, "cent": cent, "offs": striped(np.random.permutation(S)[:N])}


def reference(base, pts, cent, offs):
    idx = offs[:16].T.reshape(-1)
    q = f64(pts)
    p = f64(cent)
    na = np.sum(p * p, axis=0)[None, :]
    nb = np.sum(q * q, axis=0)[:, None]
    dot = q.T @ p
    alpha = 1.0 - 2.0 * dot + nb
    beta = 1.0 - na
    den = 1.0 - 2.0 * dot + na * nb
    sq = (alpha * alpha * na - 2.0 * alpha * beta * dot + beta * beta * nb) / (den * den)
    t = np.sqrt(sq)
    dist = np.log((1.0 + t) / (1.0 - t))
    res = f64(base).copy()
    res[:, idx] = dist * dist
    return res

@@ -1,0 +1,102 @@
+import concourse.mybir as mybir
+
+F32, BF16, U16 = mybir.dt.float32, mybir.dt.bfloat16, mybir.dt.uint16
+ALU = mybir.AluOpType
+FUNC = mybir.ActivationFunctionType
+
+P = 128
+C, S, N, D = 384, 4096, 1024, 256
+BLOCKS = C // P
+CHUNKS = D // P
+BANK = 512
+HALVES = N // BANK
+
+FLOPS = 2 * C * N * D
+
+
+def tile_distance2centroids_kernel(tc, base, pts, cent, offs, out):
+    nc = tc.nc
+    with (
+        tc.tile_pool(name="held", bufs=1) as held,
+        tc.tile_pool(name="work", bufs=BLOCKS) as work,
+        tc.psum_pool(name="banks", bufs=7) as banks,
+        tc.psum_pool(name="norms", bufs=1) as norms,
+    ):
+        offsets = held.tile([P, N // 16], U16, name="offsets")
+        nc.sync.dma_start(offsets[:], offs)
+        cent_sb = held.tile([P, CHUNKS, N], BF16, name="cent_sb")
+        nc.sync.dma_start(cent_sb[:], cent.rearrange("(k p) n -> p k n", p=P))
+        pts_sb = held.tile([P, CHUNKS, C], BF16, name="pts_sb")
+        nc.sync.dma_start(pts_sb[:], pts.rearrange("(k p) c -> p k c", p=P))
+        windows = [held.tile([P, S], F32, name=f"window{i}") for i in range(BLOCKS)]
+        for i in range(BLOCKS):
+            nc.sync.dma_start(windows[i][:], base[i * P : (i + 1) * P, :])
+
+        ones = held.tile([P, BANK], BF16, name="ones")
+        nc.gpsimd.memset(ones[:], 1.0)
+        cent_sq = held.tile([P, CHUNKS, N], BF16, name="cent_sq")
+        for h in range(HALVES):
+            cols = slice(h * BANK, (h + 1) * BANK)
+            nc.vector.tensor_tensor(cent_sq[:, :, cols], cent_sb[:, :, cols], cent_sb[:, :, cols], ALU.mult)
+        pts_sq = held.tile([P, CHUNKS, C], BF16, name="pts_sq")
+        nc.vector.tensor_tensor(pts_sq[:], pts_sb[:], pts_sb[:], ALU.mult)
+        pts_m2 = held.tile([P, CHUNKS, C], BF16, name="pts_m2")
+        nc.vector.tensor_scalar(out=pts_m2[:], in0=pts_sb[:], scalar1=-2.0, scalar2=None, op0=ALU.mult)
+
+        ln_one_minus_na = held.tile([P, N], F32, name="ln_one_minus_na")
+        inv_one_minus_na = held.tile([P, N], F32, name="inv_one_minus_na")
+        for h in range(HALVES):
+            cols = slice(h * BANK, (h + 1) * BANK)
+            na_ps = banks.tile([P, BANK], F32, name="na_ps", tag="bank")
+            for k in range(CHUNKS):
+                nc.tensor.matmul(na_ps[:], ones[:, 0:P], cent_sq[:, k, cols], start=(k == 0), stop=(k == CHUNKS - 1))
+            nc.scalar.activation(ln_one_minus_na[:, cols], na_ps[:], FUNC.Ln, bias=1.0, scale=-1.0)
+            nc.scalar.activation(inv_one_minus_na[:, cols], ln_one_minus_na[:, cols], FUNC.Exp, scale=-1.0)
+
+        nb_ps = norms.tile([P, BLOCKS], F32, name="nb_ps")
+        for i in range(BLOCKS):
+            for k in range(CHUNKS):
+                nc.tensor.matmul(
+                    nb_ps[:, i : i + 1], pts_sq[:, k, i * P : (i + 1) * P], ones[:, 0:1],
+                    start=(k == 0), stop=(k == CHUNKS - 1),
+                )
+        half_one_minus_nb = held.tile([P, BLOCKS], F32, name="half_one_minus_nb")
+        nc.vector.tensor_scalar(
+            out=half_one_minus_nb[:], in0=nb_ps[:], scalar1=-0.5, scalar2=0.5, op0=ALU.mult, op1=ALU.add
+        )
+        two_inv_one_minus_nb = held.tile([P, BLOCKS], F32, name="two_inv_one_minus_nb")
+        nc.vector.reciprocal(two_inv_one_minus_nb[:], half_one_minus_nb[:])
+
+        cosh_m1 = []
+        for i in range(BLOCKS):
+            rows = slice(i * P, (i + 1) * P)
+            cosh_m1.append(work.tile([P, N], F32, name="cosh_m1"))
+            for h in range(HALVES):
+                cols = slice(h * BANK, (h + 1) * BANK)
+                u_ps = banks.tile([P, BANK], F32, name="u_ps", tag="bank")
+                for k in range(CHUNKS):
+                    nc.tensor.matmul(u_ps[:], pts_m2[:, k, rows], cent_sb[:, k, cols], start=(k == 0), stop=False)
+                for k in range(CHUNKS):
+                    nc.tensor.matmul(u_ps[:], ones[:, 0:P], cent_sq[:, k, cols], start=False, stop=False)
+                for k in range(CHUNKS):
+                    nc.tensor.matmul(u_ps[:], pts_sq[:, k, rows], ones[:], start=False, stop=(k == CHUNKS - 1))
+                nc.vector.scalar_tensor_tensor(
+                    out=cosh_m1[i][:, cols], in0=u_ps[:], scalar=two_inv_one_minus_nb[:, i : i + 1],
+                    in1=inv_one_minus_na[:, cols], op0=ALU.mult, op1=ALU.mult,
+                )
+
+        for i in range(BLOCKS):
+            cosh_sq = work.tile([P, N], F32, name="cosh_sq")
+            ln_sinh_sq = work.tile([P, N], F32, name="ln_sinh_sq")
+            sinh = work.tile([P, N], F32, name="sinh")
+            exp_m1 = work.tile([P, N], F32, name="exp_m1")
+            dist = work.tile([P, N], F32, name="dist")
+            for h in range(HALVES):
+                cols = slice(h * BANK, (h + 1) * BANK)
+                nc.scalar.activation(cosh_sq[:, cols], cosh_m1[i][:, cols], FUNC.Square, bias=1.0)
+                nc.scalar.activation(ln_sinh_sq[:, cols], cosh_sq[:, cols], FUNC.Ln, bias=-1.0)
+                nc.scalar.activation(sinh[:, cols], ln_sinh_sq[:, cols], FUNC.Exp, scale=0.5)
+                nc.vector.tensor_tensor(exp_m1[:, cols], cosh_m1[i][:, cols], sinh[:, cols], ALU.add)
+                nc.scalar.activation(dist[:, cols], exp_m1[:, cols], FUNC.Ln, bias=1.0)
+            nc.vector.tensor_tensor(windows[i][:].indirect(offsets[:]), dist[:], dist[:], ALU.mult)
+            nc.sync.dma_start(out[i * P : (i + 1) * P, :], windows[i][:])

@@ -1,4 +1,5 @@
 import concourse.mybir as mybir
+from concourse.masks import make_identity
 
 F32, BF16, U16 = mybir.dt.float32, mybir.dt.bfloat16, mybir.dt.uint16
 ALU = mybir.AluOpType
@@ -18,8 +19,8 @@ def tile_distance2centroids_kernel(tc, base, pts, cent, offs, out):
     nc = tc.nc
     with (
         tc.tile_pool(name="held", bufs=1) as held,
-        tc.tile_pool(name="work", bufs=BLOCKS) as work,
-        tc.psum_pool(name="banks", bufs=7) as banks,
+        tc.psum_pool(name="dots", bufs=4) as dots,
+        tc.psum_pool(name="sums", bufs=3) as sums,
         tc.psum_pool(name="norms", bufs=1) as norms,
     ):
         offsets = held.tile([P, N // 16], U16, name="offsets")
@@ -32,8 +33,10 @@ def tile_distance2centroids_kernel(tc, base, pts, cent, offs, out):
         for i in range(BLOCKS):
             nc.sync.dma_start(windows[i][:], base[i * P : (i + 1) * P, :])
 
-        ones = held.tile([P, BANK], BF16, name="ones")
+        ones = held.tile([P, P], BF16, name="ones")
         nc.gpsimd.memset(ones[:], 1.0)
+        ident = held.tile([P, P], F32, name="ident")
+        make_identity(nc, ident[:])
         cent_sq = held.tile([P, CHUNKS, N], BF16, name="cent_sq")
         for h in range(HALVES):
             cols = slice(h * BANK, (h + 1) * BANK)
@@ -47,10 +50,12 @@ def tile_distance2centroids_kernel(tc, base, pts, cent, offs, out):
         inv_one_minus_na = held.tile([P, N], F32, name="inv_one_minus_na")
         for h in range(HALVES):
             cols = slice(h * BANK, (h + 1) * BANK)
-            na_ps = banks.tile([P, BANK], F32, name="na_ps", tag="bank")
+            na_ps = dots.tile([P, BANK], F32, name="na_ps", tag="dot")
             for k in range(CHUNKS):
-                nc.tensor.matmul(na_ps[:], ones[:, 0:P], cent_sq[:, k, cols], start=(k == 0), stop=(k == CHUNKS - 1))
+                nc.tensor.matmul(na_ps[:], ones[:], cent_sq[:, k, cols], start=(k == 0), stop=(k == CHUNKS - 1))
             nc.scalar.activation(ln_one_minus_na[:, cols], na_ps[:], FUNC.Ln, bias=1.0, scale=-1.0)
+        for h in range(HALVES):
+            cols = slice(h * BANK, (h + 1) * BANK)
             nc.scalar.activation(inv_one_minus_na[:, cols], ln_one_minus_na[:, cols], FUNC.Exp, scale=-1.0)
 
         nb_ps = norms.tile([P, BLOCKS], F32, name="nb_ps")
@@ -60,43 +65,58 @@ def tile_distance2centroids_kernel(tc, base, pts, cent, offs, out):
                     nb_ps[:, i : i + 1], pts_sq[:, k, i * P : (i + 1) * P], ones[:, 0:1],
                     start=(k == 0), stop=(k == CHUNKS - 1),
                 )
-        half_one_minus_nb = held.tile([P, BLOCKS], F32, name="half_one_minus_nb")
-        nc.vector.tensor_scalar(
-            out=half_one_minus_nb[:], in0=nb_ps[:], scalar1=-0.5, scalar2=0.5, op0=ALU.mult, op1=ALU.add
-        )
-        two_inv_one_minus_nb = held.tile([P, BLOCKS], F32, name="two_inv_one_minus_nb")
-        nc.vector.reciprocal(two_inv_one_minus_nb[:], half_one_minus_nb[:])
+        one_plus_nb = held.tile([P, BLOCKS], F32, name="one_plus_nb")
+        nc.vector.tensor_scalar(out=one_plus_nb[:], in0=nb_ps[:], scalar1=1.0, scalar2=None, op0=ALU.add)
+        inv_r = held.tile([P, BLOCKS], F32, name="inv_r")
+        nc.vector.tensor_scalar(out=inv_r[:], in0=nb_ps[:], scalar1=-0.5, scalar2=0.5, op0=ALU.mult, op1=ALU.add)
+        r = held.tile([P, BLOCKS], F32, name="r")
+        nc.vector.reciprocal(r[:], inv_r[:])
+        one_minus_r = held.tile([P, BLOCKS], F32, name="one_minus_r")
+        nc.vector.tensor_scalar(out=one_minus_r[:], in0=r[:], scalar1=-1.0, scalar2=1.0, op0=ALU.mult, op1=ALU.add)
+        r_sq = held.tile([P, BLOCKS], F32, name="r_sq")
+        nc.vector.tensor_tensor(r_sq[:], r[:], r[:], ALU.mult)
+        r_sq_nb = held.tile([P, BLOCKS], F32, name="r_sq_nb")
+        nc.vector.tensor_tensor(r_sq_nb[:], r_sq[:], nb_ps[:], ALU.mult)
+        diag_r = held.tile([P, BLOCKS, P], F32, name="diag_r")
+        for i in range(BLOCKS):
+            nc.vector.tensor_scalar(
+                out=diag_r[:, i, :], in0=ident[:], scalar1=r[:, i : i + 1], scalar2=None, op0=ALU.mult
+            )
 
-        cosh_m1 = []
+        y = [held.tile([P, N], F32, name=f"y{i}") for i in range(BLOCKS)]
+        y_poly = [held.tile([P, N], F32, name=f"y_poly{i}") for i in range(BLOCKS)]
         for i in range(BLOCKS):
             rows = slice(i * P, (i + 1) * P)
-            cosh_m1.append(work.tile([P, N], F32, name="cosh_m1"))
             for h in range(HALVES):
                 cols = slice(h * BANK, (h + 1) * BANK)
-                u_ps = banks.tile([P, BANK], F32, name="u_ps", tag="bank")
+                dot_ps = dots.tile([P, BANK], F32, name="dot_ps", tag="dot")
                 for k in range(CHUNKS):
-                    nc.tensor.matmul(u_ps[:], pts_m2[:, k, rows], cent_sb[:, k, cols], start=(k == 0), stop=False)
-                for k in range(CHUNKS):
-                    nc.tensor.matmul(u_ps[:], ones[:, 0:P], cent_sq[:, k, cols], start=False, stop=False)
-                for k in range(CHUNKS):
-                    nc.tensor.matmul(u_ps[:], pts_sq[:, k, rows], ones[:], start=False, stop=(k == CHUNKS - 1))
+                    nc.tensor.matmul(
+                        dot_ps[:], pts_m2[:, k, rows], cent_sb[:, k, cols], start=(k == 0), stop=(k == CHUNKS - 1)
+                    )
                 nc.vector.scalar_tensor_tensor(
-                    out=cosh_m1[i][:, cols], in0=u_ps[:], scalar=two_inv_one_minus_nb[:, i : i + 1],
-                    in1=inv_one_minus_na[:, cols], op0=ALU.mult, op1=ALU.mult,
+                    out=y[i][:, cols], in0=dot_ps[:], scalar=one_plus_nb[:, i : i + 1],
+                    in1=inv_one_minus_na[:, cols], op0=ALU.add, op1=ALU.mult,
+                )
+                nc.vector.scalar_tensor_tensor(
+                    out=y_poly[i][:, cols], in0=y[i][:, cols], scalar=one_plus_nb[:, i : i + 1],
+                    in1=y[i][:, cols], op0=ALU.subtract, op1=ALU.mult,
                 )
 
         for i in range(BLOCKS):
-            cosh_sq = work.tile([P, N], F32, name="cosh_sq")
-            ln_sinh_sq = work.tile([P, N], F32, name="ln_sinh_sq")
-            sinh = work.tile([P, N], F32, name="sinh")
-            exp_m1 = work.tile([P, N], F32, name="exp_m1")
-            dist = work.tile([P, N], F32, name="dist")
+            sinh = held.tile([P, N], F32, name="sinh", tag="sinh")
+            dist = held.tile([P, N], F32, name=f"dist{i}")
             for h in range(HALVES):
                 cols = slice(h * BANK, (h + 1) * BANK)
-                nc.scalar.activation(cosh_sq[:, cols], cosh_m1[i][:, cols], FUNC.Square, bias=1.0)
-                nc.scalar.activation(ln_sinh_sq[:, cols], cosh_sq[:, cols], FUNC.Ln, bias=-1.0)
-                nc.scalar.activation(sinh[:, cols], ln_sinh_sq[:, cols], FUNC.Exp, scale=0.5)
-                nc.vector.tensor_tensor(exp_m1[:, cols], cosh_m1[i][:, cols], sinh[:, cols], ALU.add)
-                nc.scalar.activation(dist[:, cols], exp_m1[:, cols], FUNC.Ln, bias=1.0)
+                nc.scalar.activation(
+                    sinh[:, cols], y_poly[i][:, cols], FUNC.Sqrt,
+                    bias=r_sq_nb[:, i : i + 1], scale=r_sq[:, i : i + 1],
+                )
+            for h in range(HALVES):
+                cols = slice(h * BANK, (h + 1) * BANK)
+                sum_ps = sums.tile([P, BANK], F32, name="sum_ps", tag="sum")
+                nc.tensor.matmul(sum_ps[:], diag_r[:, i, :], y[i][:, cols], start=True, stop=False)
+                nc.tensor.matmul(sum_ps[:], ident[:], sinh[:, cols], start=False, stop=True)
+                nc.scalar.activation(dist[:, cols], sum_ps[:], FUNC.Ln, bias=one_minus_r[:, i : i + 1])
             nc.vector.tensor_tensor(windows[i][:].indirect(offsets[:]), dist[:], dist[:], ALU.mult)
             nc.sync.dma_start(out[i * P : (i + 1) * P, :], windows[i][:])

@@ -12,6 +12,8 @@ CHUNKS = D // P
 BANK = 512
 HALVES = N // BANK
 
+WARM_UPS = 4
+
 FLOPS = 2 * C * N * D
 
 
@@ -19,22 +21,27 @@ def tile_distance2centroids_kernel(tc, base, pts, cent, offs, out):
     nc = tc.nc
     with (
         tc.tile_pool(name="held", bufs=1) as held,
-        tc.psum_pool(name="dots", bufs=4) as dots,
-        tc.psum_pool(name="sums", bufs=3) as sums,
+        tc.psum_pool(name="dots", bufs=5) as dots,
+        tc.psum_pool(name="sums", bufs=2) as sums,
         tc.psum_pool(name="norms", bufs=1) as norms,
     ):
+        cent_sb = held.tile([P, CHUNKS, N], BF16, name="cent_sb")
+        cent_chunks = cent.rearrange("(k p) n -> p k n", p=P)
+        nc.sync.dma_start(cent_sb[:, :, 0:BANK], cent_chunks[:, :, 0:BANK])
+        nc.scalar.dma_start(cent_sb[:, :, BANK:N], cent_chunks[:, :, BANK:N])
+        pts_sb = held.tile([P, CHUNKS, C], BF16, name="pts_sb")
+        nc.scalar.dma_start(pts_sb[:], pts.rearrange("(k p) c -> p k c", p=P))
         offsets = held.tile([P, N // 16], U16, name="offsets")
         nc.sync.dma_start(offsets[:], offs)
-        cent_sb = held.tile([P, CHUNKS, N], BF16, name="cent_sb")
-        nc.sync.dma_start(cent_sb[:], cent.rearrange("(k p) n -> p k n", p=P))
-        pts_sb = held.tile([P, CHUNKS, C], BF16, name="pts_sb")
-        nc.sync.dma_start(pts_sb[:], pts.rearrange("(k p) c -> p k c", p=P))
         windows = [held.tile([P, S], F32, name=f"window{i}") for i in range(BLOCKS)]
         for i in range(BLOCKS):
             nc.sync.dma_start(windows[i][:], base[i * P : (i + 1) * P, :])
 
-        ones = held.tile([P, P], BF16, name="ones")
-        nc.gpsimd.memset(ones[:], 1.0)
+        ones = held.tile([P, BANK], BF16, name="ones")
+        nc.vector.memset(ones[:], 1.0)
+        warm_ps = dots.tile([P, BANK], F32, name="warm_ps", tag="dot")
+        for w in range(WARM_UPS):
+            nc.tensor.matmul(warm_ps[:], ones[:, 0:P], ones[:], start=True, stop=True)
         ident = held.tile([P, P], F32, name="ident")
         make_identity(nc, ident[:])
         cent_sq = held.tile([P, CHUNKS, N], BF16, name="cent_sq")
@@ -46,17 +53,19 @@ def tile_distance2centroids_kernel(tc, base, pts, cent, offs, out):
         pts_m2 = held.tile([P, CHUNKS, C], BF16, name="pts_m2")
         nc.vector.tensor_scalar(out=pts_m2[:], in0=pts_sb[:], scalar1=-2.0, scalar2=None, op0=ALU.mult)
 
-        ln_one_minus_na = held.tile([P, N], F32, name="ln_one_minus_na")
+        rsqrt_one_minus_na = held.tile([P, N], F32, name="rsqrt_one_minus_na")
         inv_one_minus_na = held.tile([P, N], F32, name="inv_one_minus_na")
         for h in range(HALVES):
             cols = slice(h * BANK, (h + 1) * BANK)
             na_ps = dots.tile([P, BANK], F32, name="na_ps", tag="dot")
             for k in range(CHUNKS):
-                nc.tensor.matmul(na_ps[:], ones[:], cent_sq[:, k, cols], start=(k == 0), stop=(k == CHUNKS - 1))
-            nc.scalar.activation(ln_one_minus_na[:, cols], na_ps[:], FUNC.Ln, bias=1.0, scale=-1.0)
+                nc.tensor.matmul(na_ps[:], ones[:, 0:P], cent_sq[:, k, cols], start=(k == 0), stop=(k == CHUNKS - 1))
+            nc.scalar.activation(
+                rsqrt_one_minus_na[:, cols], na_ps[:], FUNC.Abs_reciprocal_sqrt, bias=1.0, scale=-1.0
+            )
         for h in range(HALVES):
             cols = slice(h * BANK, (h + 1) * BANK)
-            nc.scalar.activation(inv_one_minus_na[:, cols], ln_one_minus_na[:, cols], FUNC.Exp, scale=-1.0)
+            nc.scalar.activation(inv_one_minus_na[:, cols], rsqrt_one_minus_na[:, cols], FUNC.Square)
 
         nb_ps = norms.tile([P, BLOCKS], F32, name="nb_ps")
         for i in range(BLOCKS):
@@ -65,6 +74,8 @@ def tile_distance2centroids_kernel(tc, base, pts, cent, offs, out):
                     nb_ps[:, i : i + 1], pts_sq[:, k, i * P : (i + 1) * P], ones[:, 0:1],
                     start=(k == 0), stop=(k == CHUNKS - 1),
                 )
+        nb = held.tile([P, BLOCKS], F32, name="nb")
+        nc.vector.tensor_copy(nb[:], nb_ps[:])
         one_plus_nb = held.tile([P, BLOCKS], F32, name="one_plus_nb")
         nc.vector.tensor_scalar(out=one_plus_nb[:], in0=nb_ps[:], scalar1=1.0, scalar2=None, op0=ALU.add)
         inv_r = held.tile([P, BLOCKS], F32, name="inv_r")
@@ -73,15 +84,6 @@ def tile_distance2centroids_kernel(tc, base, pts, cent, offs, out):
         nc.vector.reciprocal(r[:], inv_r[:])
         one_minus_r = held.tile([P, BLOCKS], F32, name="one_minus_r")
         nc.vector.tensor_scalar(out=one_minus_r[:], in0=r[:], scalar1=-1.0, scalar2=1.0, op0=ALU.mult, op1=ALU.add)
-        r_sq = held.tile([P, BLOCKS], F32, name="r_sq")
-        nc.vector.tensor_tensor(r_sq[:], r[:], r[:], ALU.mult)
-        r_sq_nb = held.tile([P, BLOCKS], F32, name="r_sq_nb")
-        nc.vector.tensor_tensor(r_sq_nb[:], r_sq[:], nb_ps[:], ALU.mult)
-        diag_r = held.tile([P, BLOCKS, P], F32, name="diag_r")
-        for i in range(BLOCKS):
-            nc.vector.tensor_scalar(
-                out=diag_r[:, i, :], in0=ident[:], scalar1=r[:, i : i + 1], scalar2=None, op0=ALU.mult
-            )
 
         y = [held.tile([P, N], F32, name=f"y{i}") for i in range(BLOCKS)]
         y_poly = [held.tile([P, N], F32, name=f"y_poly{i}") for i in range(BLOCKS)]
@@ -98,25 +100,24 @@ def tile_distance2centroids_kernel(tc, base, pts, cent, offs, out):
                     out=y[i][:, cols], in0=dot_ps[:], scalar=one_plus_nb[:, i : i + 1],
                     in1=inv_one_minus_na[:, cols], op0=ALU.add, op1=ALU.mult,
                 )
-                nc.vector.scalar_tensor_tensor(
-                    out=y_poly[i][:, cols], in0=y[i][:, cols], scalar=one_plus_nb[:, i : i + 1],
-                    in1=y[i][:, cols], op0=ALU.subtract, op1=ALU.mult,
-                )
+            nc.vector.scalar_tensor_tensor(
+                out=y_poly[i][:], in0=y[i][:], scalar=one_plus_nb[:, i : i + 1], in1=y[i][:],
+                op0=ALU.subtract, op1=ALU.mult,
+            )
 
         for i in range(BLOCKS):
-            sinh = held.tile([P, N], F32, name="sinh", tag="sinh")
+            root = held.tile([P, N], F32, name="root", tag="root")
             dist = held.tile([P, N], F32, name=f"dist{i}")
             for h in range(HALVES):
                 cols = slice(h * BANK, (h + 1) * BANK)
-                nc.scalar.activation(
-                    sinh[:, cols], y_poly[i][:, cols], FUNC.Sqrt,
-                    bias=r_sq_nb[:, i : i + 1], scale=r_sq[:, i : i + 1],
-                )
+                nc.scalar.activation(root[:, cols], y_poly[i][:, cols], FUNC.Sqrt, bias=nb[:, i : i + 1])
             for h in range(HALVES):
                 cols = slice(h * BANK, (h + 1) * BANK)
                 sum_ps = sums.tile([P, BANK], F32, name="sum_ps", tag="sum")
-                nc.tensor.matmul(sum_ps[:], diag_r[:, i, :], y[i][:, cols], start=True, stop=False)
-                nc.tensor.matmul(sum_ps[:], ident[:], sinh[:, cols], start=False, stop=True)
-                nc.scalar.activation(dist[:, cols], sum_ps[:], FUNC.Ln, bias=one_minus_r[:, i : i + 1])
+                nc.tensor.matmul(sum_ps[:], ident[:], y[i][:, cols], start=True, stop=False)
+                nc.tensor.matmul(sum_ps[:], ident[:], root[:, cols], start=False, stop=True)
+                nc.scalar.activation(
+                    dist[:, cols], sum_ps[:], FUNC.Ln, bias=one_minus_r[:, i : i + 1], scale=r[:, i : i + 1]
+                )
             nc.vector.tensor_tensor(windows[i][:].indirect(offsets[:]), dist[:], dist[:], ALU.mult)
             nc.sync.dma_start(out[i * P : (i + 1) * P, :], windows[i][:])

@@ -28,9 +28,9 @@ def tile_distance2centroids_kernel(tc, base, pts, cent, offs, out):
         cent_sb = held.tile([P, CHUNKS, N], BF16, name="cent_sb")
         cent_chunks = cent.rearrange("(k p) n -> p k n", p=P)
         nc.sync.dma_start(cent_sb[:, :, 0:BANK], cent_chunks[:, :, 0:BANK])
-        nc.scalar.dma_start(cent_sb[:, :, BANK:N], cent_chunks[:, :, BANK:N])
+        nc.sync.dma_start(cent_sb[:, :, BANK:N], cent_chunks[:, :, BANK:N])
         pts_sb = held.tile([P, CHUNKS, C], BF16, name="pts_sb")
-        nc.scalar.dma_start(pts_sb[:], pts.rearrange("(k p) c -> p k c", p=P))
+        nc.sync.dma_start(pts_sb[:], pts.rearrange("(k p) c -> p k c", p=P))
         offsets = held.tile([P, N // 16], U16, name="offsets")
         nc.sync.dma_start(offsets[:], offs)
         windows = [held.tile([P, S], F32, name=f"window{i}") for i in range(BLOCKS)]
@@ -63,8 +63,6 @@ def tile_distance2centroids_kernel(tc, base, pts, cent, offs, out):
             nc.scalar.activation(
                 rsqrt_one_minus_na[:, cols], na_ps[:], FUNC.Abs_reciprocal_sqrt, bias=1.0, scale=-1.0
             )
-        for h in range(HALVES):
-            cols = slice(h * BANK, (h + 1) * BANK)
             nc.scalar.activation(inv_one_minus_na[:, cols], rsqrt_one_minus_na[:, cols], FUNC.Square)
 
         nb_ps = norms.tile([P, BLOCKS], F32, name="nb_ps")
@@ -100,10 +98,10 @@ def tile_distance2centroids_kernel(tc, base, pts, cent, offs, out):
                     out=y[i][:, cols], in0=dot_ps[:], scalar=one_plus_nb[:, i : i + 1],
                     in1=inv_one_minus_na[:, cols], op0=ALU.add, op1=ALU.mult,
                 )
-            nc.vector.scalar_tensor_tensor(
-                out=y_poly[i][:], in0=y[i][:], scalar=one_plus_nb[:, i : i + 1], in1=y[i][:],
-                op0=ALU.subtract, op1=ALU.mult,
-            )
+                nc.vector.scalar_tensor_tensor(
+                    out=y_poly[i][:, cols], in0=y[i][:, cols], scalar=one_plus_nb[:, i : i + 1],
+                    in1=y[i][:, cols], op0=ALU.subtract, op1=ALU.mult,
+                )
 
         for i in range(BLOCKS):
             root = held.tile([P, N], F32, name="root", tag="root")

@@ -28,9 +28,9 @@ def tile_distance2centroids_kernel(tc, base, pts, cent, offs, out):
         cent_sb = held.tile([P, CHUNKS, N], BF16, name="cent_sb")
         cent_chunks = cent.rearrange("(k p) n -> p k n", p=P)
         nc.sync.dma_start(cent_sb[:, :, 0:BANK], cent_chunks[:, :, 0:BANK])
-        nc.sync.dma_start(cent_sb[:, :, BANK:N], cent_chunks[:, :, BANK:N])
+        nc.scalar.dma_start(cent_sb[:, :, BANK:N], cent_chunks[:, :, BANK:N])
         pts_sb = held.tile([P, CHUNKS, C], BF16, name="pts_sb")
-        nc.sync.dma_start(pts_sb[:], pts.rearrange("(k p) c -> p k c", p=P))
+        nc.scalar.dma_start(pts_sb[:], pts.rearrange("(k p) c -> p k c", p=P))
         offsets = held.tile([P, N // 16], U16, name="offsets")
         nc.sync.dma_start(offsets[:], offs)
         windows = [held.tile([P, S], F32, name=f"window{i}") for i in range(BLOCKS)]

@@ -12,8 +12,6 @@ CHUNKS = D // P
 BANK = 512
 HALVES = N // BANK
 
-WARM_UPS = 4
-
 FLOPS = 2 * C * N * D
 
 
@@ -28,20 +26,17 @@ def tile_distance2centroids_kernel(tc, base, pts, cent, offs, out):
         cent_sb = held.tile([P, CHUNKS, N], BF16, name="cent_sb")
         cent_chunks = cent.rearrange("(k p) n -> p k n", p=P)
         nc.sync.dma_start(cent_sb[:, :, 0:BANK], cent_chunks[:, :, 0:BANK])
-        nc.scalar.dma_start(cent_sb[:, :, BANK:N], cent_chunks[:, :, BANK:N])
+        nc.sync.dma_start(cent_sb[:, :, BANK:N], cent_chunks[:, :, BANK:N])
         pts_sb = held.tile([P, CHUNKS, C], BF16, name="pts_sb")
-        nc.scalar.dma_start(pts_sb[:], pts.rearrange("(k p) c -> p k c", p=P))
+        nc.sync.dma_start(pts_sb[:], pts.rearrange("(k p) c -> p k c", p=P))
         offsets = held.tile([P, N // 16], U16, name="offsets")
         nc.sync.dma_start(offsets[:], offs)
         windows = [held.tile([P, S], F32, name=f"window{i}") for i in range(BLOCKS)]
         for i in range(BLOCKS):
             nc.sync.dma_start(windows[i][:], base[i * P : (i + 1) * P, :])
 
-        ones = held.tile([P, BANK], BF16, name="ones")
+        ones = held.tile([P, P], BF16, name="ones")
         nc.vector.memset(ones[:], 1.0)
-        warm_ps = dots.tile([P, BANK], F32, name="warm_ps", tag="dot")
-        for w in range(WARM_UPS):
-            nc.tensor.matmul(warm_ps[:], ones[:, 0:P], ones[:], start=True, stop=True)
         ident = held.tile([P, P], F32, name="ident")
         make_identity(nc, ident[:])
         cent_sq = held.tile([P, CHUNKS, N], BF16, name="cent_sq")
@@ -59,7 +54,7 @@ def tile_distance2centroids_kernel(tc, base, pts, cent, offs, out):
             cols = slice(h * BANK, (h + 1) * BANK)
             na_ps = dots.tile([P, BANK], F32, name="na_ps", tag="dot")
             for k in range(CHUNKS):
-                nc.tensor.matmul(na_ps[:], ones[:, 0:P], cent_sq[:, k, cols], start=(k == 0), stop=(k == CHUNKS - 1))
+                nc.tensor.matmul(na_ps[:], ones[:], cent_sq[:, k, cols], start=(k == 0), stop=(k == CHUNKS - 1))
             nc.scalar.activation(
                 rsqrt_one_minus_na[:, cols], na_ps[:], FUNC.Abs_reciprocal_sqrt, bias=1.0, scale=-1.0
             )

@@ -12,6 +12,8 @@ CHUNKS = D // P
 BANK = 512
 HALVES = N // BANK
 
+WARM_UPS = 4
+
 FLOPS = 2 * C * N * D
 
 
@@ -35,8 +37,11 @@ def tile_distance2centroids_kernel(tc, base, pts, cent, offs, out):
         for i in range(BLOCKS):
             nc.sync.dma_start(windows[i][:], base[i * P : (i + 1) * P, :])
 
-        ones = held.tile([P, P], BF16, name="ones")
+        ones = held.tile([P, BANK], BF16, name="ones")
         nc.vector.memset(ones[:], 1.0)
+        warm_ps = dots.tile([P, BANK], F32, name="warm_ps", tag="dot")
+        for w in range(WARM_UPS):
+            nc.tensor.matmul(warm_ps[:], ones[:, 0:P], ones[:], start=True, stop=True)
         ident = held.tile([P, P], F32, name="ident")
         make_identity(nc, ident[:])
         cent_sq = held.tile([P, CHUNKS, N], BF16, name="cent_sq")
@@ -54,11 +59,13 @@ def tile_distance2centroids_kernel(tc, base, pts, cent, offs, out):
             cols = slice(h * BANK, (h + 1) * BANK)
             na_ps = dots.tile([P, BANK], F32, name="na_ps", tag="dot")
             for k in range(CHUNKS):
-                nc.tensor.matmul(na_ps[:], ones[:], cent_sq[:, k, cols], start=(k == 0), stop=(k == CHUNKS - 1))
+                nc.tensor.matmul(na_ps[:], ones[:, 0:P], cent_sq[:, k, cols], start=(k == 0), stop=(k == CHUNKS - 1))
             nc.scalar.activation(
                 rsqrt_one_minus_na[:, cols], na_ps[:], FUNC.Abs_reciprocal_sqrt, bias=1.0, scale=-1.0
             )
-            nc.scalar.activation(inv_one_minus_na[:, cols], rsqrt_one_minus_na[:, cols], FUNC.Square)
+            nc.vector.tensor_tensor(
+                inv_one_minus_na[:, cols], rsqrt_one_minus_na[:, cols], rsqrt_one_minus_na[:, cols], ALU.mult
+            )
 
         nb_ps = norms.tile([P, BLOCKS], F32, name="nb_ps")
         for i in range(BLOCKS):
@@ -71,15 +78,23 @@ def tile_distance2centroids_kernel(tc, base, pts, cent, offs, out):
         nc.vector.tensor_copy(nb[:], nb_ps[:])
         one_plus_nb = held.tile([P, BLOCKS], F32, name="one_plus_nb")
         nc.vector.tensor_scalar(out=one_plus_nb[:], in0=nb_ps[:], scalar1=1.0, scalar2=None, op0=ALU.add)
+        minus_half_one_plus_nb = held.tile([P, BLOCKS], F32, name="minus_half_one_plus_nb")
+        nc.vector.tensor_scalar(
+            out=minus_half_one_plus_nb[:], in0=nb_ps[:], scalar1=-0.5, scalar2=-0.5, op0=ALU.mult, op1=ALU.add
+        )
         inv_r = held.tile([P, BLOCKS], F32, name="inv_r")
         nc.vector.tensor_scalar(out=inv_r[:], in0=nb_ps[:], scalar1=-0.5, scalar2=0.5, op0=ALU.mult, op1=ALU.add)
+        minus_inv_r_sq = held.tile([P, BLOCKS], F32, name="minus_inv_r_sq")
+        nc.vector.scalar_tensor_tensor(
+            out=minus_inv_r_sq[:], in0=inv_r[:], scalar=-1.0, in1=inv_r[:], op0=ALU.mult, op1=ALU.mult
+        )
         r = held.tile([P, BLOCKS], F32, name="r")
         nc.vector.reciprocal(r[:], inv_r[:])
         one_minus_r = held.tile([P, BLOCKS], F32, name="one_minus_r")
         nc.vector.tensor_scalar(out=one_minus_r[:], in0=r[:], scalar1=-1.0, scalar2=1.0, op0=ALU.mult, op1=ALU.add)
 
         y = [held.tile([P, N], F32, name=f"y{i}") for i in range(BLOCKS)]
-        y_poly = [held.tile([P, N], F32, name=f"y_poly{i}") for i in range(BLOCKS)]
+        y_poly = [held.tile([P, N], F32, name=f"y_poly{i}") for i in range(BLOCKS - 1)]
         for i in range(BLOCKS):
             rows = slice(i * P, (i + 1) * P)
             for h in range(HALVES):
@@ -93,17 +108,27 @@ def tile_distance2centroids_kernel(tc, base, pts, cent, offs, out):
                     out=y[i][:, cols], in0=dot_ps[:], scalar=one_plus_nb[:, i : i + 1],
                     in1=inv_one_minus_na[:, cols], op0=ALU.add, op1=ALU.mult,
                 )
-                nc.vector.scalar_tensor_tensor(
-                    out=y_poly[i][:, cols], in0=y[i][:, cols], scalar=one_plus_nb[:, i : i + 1],
-                    in1=y[i][:, cols], op0=ALU.subtract, op1=ALU.mult,
-                )
+                if i < BLOCKS - 1:
+                    nc.vector.scalar_tensor_tensor(
+                        out=y_poly[i][:, cols], in0=y[i][:, cols], scalar=one_plus_nb[:, i : i + 1],
+                        in1=y[i][:, cols], op0=ALU.subtract, op1=ALU.mult,
+                    )
 
         for i in range(BLOCKS):
             root = held.tile([P, N], F32, name="root", tag="root")
             dist = held.tile([P, N], F32, name=f"dist{i}")
+            if i < BLOCKS - 1:
+                under_root, rest = y_poly[i], nb
+            else:
+                under_root, rest = root, minus_inv_r_sq
+                for h in range(HALVES):
+                    cols = slice(h * BANK, (h + 1) * BANK)
+                    nc.scalar.activation(
+                        root[:, cols], y[i][:, cols], FUNC.Square, bias=minus_half_one_plus_nb[:, i : i + 1]
+                    )
             for h in range(HALVES):
                 cols = slice(h * BANK, (h + 1) * BANK)
-                nc.scalar.activation(root[:, cols], y_poly[i][:, cols], FUNC.Sqrt, bias=nb[:, i : i + 1])
+                nc.scalar.activation(root[:, cols], under_root[:, cols], FUNC.Sqrt, bias=rest[:, i : i + 1])
             for h in range(HALVES):
                 cols = slice(h * BANK, (h + 1) * BANK)
                 sum_ps = sums.tile([P, BANK], F32, name="sum_ps", tag="sum")

@@ -137,5 +137,8 @@ def tile_distance2centroids_kernel(tc, base, pts, cent, offs, out):
                 nc.scalar.activation(
                     dist[:, cols], sum_ps[:], FUNC.Ln, bias=one_minus_r[:, i : i + 1], scale=r[:, i : i + 1]
                 )
-            nc.vector.tensor_tensor(windows[i][:].indirect(offsets[:]), dist[:], dist[:], ALU.mult)
+            for h in range(HALVES):
+                cols = slice(h * BANK, (h + 1) * BANK)
+                piece = offsets[:, h * (BANK // 16) : (h + 1) * (BANK // 16)]
+                nc.vector.tensor_tensor(windows[i][:].indirect(piece), dist[:, cols], dist[:, cols], ALU.mult)
             nc.sync.dma_start(out[i * P : (i + 1) * P, :], windows[i][:])

@@ -63,9 +63,6 @@ def tile_distance2centroids_kernel(tc, base, pts, cent, offs, out):
             nc.scalar.activation(
                 rsqrt_one_minus_na[:, cols], na_ps[:], FUNC.Abs_reciprocal_sqrt, bias=1.0, scale=-1.0
             )
-            nc.vector.tensor_tensor(
-                inv_one_minus_na[:, cols], rsqrt_one_minus_na[:, cols], rsqrt_one_minus_na[:, cols], ALU.mult
-            )
 
         nb_ps = norms.tile([P, BLOCKS], F32, name="nb_ps")
         for i in range(BLOCKS):
@@ -93,12 +90,21 @@ def tile_distance2centroids_kernel(tc, base, pts, cent, offs, out):
         one_minus_r = held.tile([P, BLOCKS], F32, name="one_minus_r")
         nc.vector.tensor_scalar(out=one_minus_r[:], in0=r[:], scalar1=-1.0, scalar2=1.0, op0=ALU.mult, op1=ALU.add)
 
+        pairs = [[(i, h) for i in range(BLOCKS - 1)] for h in range(HALVES)]
+        pairs.append([(BLOCKS - 1, h) for h in range(HALVES)])
+
         y = [held.tile([P, N], F32, name=f"y{i}") for i in range(BLOCKS)]
         y_poly = [held.tile([P, N], F32, name=f"y_poly{i}") for i in range(BLOCKS - 1)]
-        for i in range(BLOCKS):
-            rows = slice(i * P, (i + 1) * P)
-            for h in range(HALVES):
+        squared_halves = []
+        for pair in pairs:
+            for i, h in pair:
+                rows = slice(i * P, (i + 1) * P)
                 cols = slice(h * BANK, (h + 1) * BANK)
+                if h not in squared_halves:
+                    squared_halves.append(h)
+                    nc.vector.tensor_tensor(
+                        inv_one_minus_na[:, cols], rsqrt_one_minus_na[:, cols], rsqrt_one_minus_na[:, cols], ALU.mult
+                    )
                 dot_ps = dots.tile([P, BANK], F32, name="dot_ps", tag="dot")
                 for k in range(CHUNKS):
                     nc.tensor.matmul(
@@ -114,31 +120,29 @@ def tile_distance2centroids_kernel(tc, base, pts, cent, offs, out):
                         in1=y[i][:, cols], op0=ALU.subtract, op1=ALU.mult,
                     )
 
-        for i in range(BLOCKS):
-            root = held.tile([P, N], F32, name="root", tag="root")
-            dist = held.tile([P, N], F32, name=f"dist{i}")
-            if i < BLOCKS - 1:
-                under_root, rest = y_poly[i], nb
-            else:
-                under_root, rest = root, minus_inv_r_sq
-                for h in range(HALVES):
-                    cols = slice(h * BANK, (h + 1) * BANK)
-                    nc.scalar.activation(
-                        root[:, cols], y[i][:, cols], FUNC.Square, bias=minus_half_one_plus_nb[:, i : i + 1]
-                    )
-            for h in range(HALVES):
+        dist = [held.tile([P, N], F32, name=f"dist{i}") for i in range(BLOCKS)]
+        for pair in pairs:
+            root = held.tile([P, len(pair), BANK], F32, name="root", tag="root")
+            for q, (i, h) in enumerate(pair):
                 cols = slice(h * BANK, (h + 1) * BANK)
-                nc.scalar.activation(root[:, cols], under_root[:, cols], FUNC.Sqrt, bias=rest[:, i : i + 1])
-            for h in range(HALVES):
+                if i < BLOCKS - 1:
+                    nc.scalar.activation(root[:, q, :], y_poly[i][:, cols], FUNC.Sqrt, bias=nb[:, i : i + 1])
+                else:
+                    nc.scalar.activation(
+                        root[:, q, :], y[i][:, cols], FUNC.Square, bias=minus_half_one_plus_nb[:, i : i + 1]
+                    )
+                    nc.scalar.activation(root[:, q, :], root[:, q, :], FUNC.Sqrt, bias=minus_inv_r_sq[:, i : i + 1])
+            for q, (i, h) in enumerate(pair):
                 cols = slice(h * BANK, (h + 1) * BANK)
                 sum_ps = sums.tile([P, BANK], F32, name="sum_ps", tag="sum")
                 nc.tensor.matmul(sum_ps[:], ident[:], y[i][:, cols], start=True, stop=False)
-                nc.tensor.matmul(sum_ps[:], ident[:], root[:, cols], start=False, stop=True)
+                nc.tensor.matmul(sum_ps[:], ident[:], root[:, q, :], start=False, stop=True)
                 nc.scalar.activation(
-                    dist[:, cols], sum_ps[:], FUNC.Ln, bias=one_minus_r[:, i : i + 1], scale=r[:, i : i + 1]
+                    dist[i][:, cols], sum_ps[:], FUNC.Ln, bias=one_minus_r[:, i : i + 1], scale=r[:, i : i + 1]
                 )
-            for h in range(HALVES):
+            for i, h in pair:
                 cols = slice(h * BANK, (h + 1) * BANK)
                 piece = offsets[:, h * (BANK // 16) : (h + 1) * (BANK // 16)]
-                nc.vector.tensor_tensor(windows[i][:].indirect(piece), dist[:, cols], dist[:, cols], ALU.mult)
-            nc.sync.dma_start(out[i * P : (i + 1) * P, :], windows[i][:])
+                nc.vector.tensor_tensor(windows[i][:].indirect(piece), dist[i][:, cols], dist[i][:, cols], ALU.mult)
+                if h == HALVES - 1:
+                    nc.sync.dma_start(out[i * P : (i + 1) * P, :], windows[i][:])

@@ -26,9 +26,10 @@ def tile_distance2centroids_kernel(tc, base, pts, cent, offs, out):
         tc.psum_pool(name="norms", bufs=1) as norms,
     ):
         cent_sb = held.tile([P, CHUNKS, N], BF16, name="cent_sb")
-        cent_chunks = cent.rearrange("(k p) n -> p k n", p=P)
-        nc.sync.dma_start(cent_sb[:, :, 0:BANK], cent_chunks[:, :, 0:BANK])
-        nc.sync.dma_start(cent_sb[:, :, BANK:N], cent_chunks[:, :, BANK:N])
+        for h in range(HALVES):
+            cols = slice(h * BANK, (h + 1) * BANK)
+            for k in range(CHUNKS):
+                nc.sync.dma_start(cent_sb[:, k, cols], cent[k * P : (k + 1) * P, cols])
         pts_sb = held.tile([P, CHUNKS, C], BF16, name="pts_sb")
         nc.sync.dma_start(pts_sb[:], pts.rearrange("(k p) c -> p k c", p=P))
         offsets = held.tile([P, N // 16], U16, name="offsets")
@@ -47,7 +48,8 @@ def tile_distance2centroids_kernel(tc, base, pts, cent, offs, out):
         cent_sq = held.tile([P, CHUNKS, N], BF16, name="cent_sq")
         for h in range(HALVES):
             cols = slice(h * BANK, (h + 1) * BANK)
-            nc.vector.tensor_tensor(cent_sq[:, :, cols], cent_sb[:, :, cols], cent_sb[:, :, cols], ALU.mult)
+            for k in range(CHUNKS):
+                nc.vector.tensor_tensor(cent_sq[:, k, cols], cent_sb[:, k, cols], cent_sb[:, k, cols], ALU.mult)
         pts_sq = held.tile([P, CHUNKS, C], BF16, name="pts_sq")
         nc.vector.tensor_tensor(pts_sq[:], pts_sb[:], pts_sb[:], ALU.mult)
         pts_m2 = held.tile([P, CHUNKS, C], BF16, name="pts_m2")
@@ -63,6 +65,10 @@ def tile_distance2centroids_kernel(tc, base, pts, cent, offs, out):
             nc.scalar.activation(
                 rsqrt_one_minus_na[:, cols], na_ps[:], FUNC.Abs_reciprocal_sqrt, bias=1.0, scale=-1.0
             )
+        nc.vector.tensor_tensor(
+            inv_one_minus_na[:, 0:BANK], rsqrt_one_minus_na[:, 0:BANK], rsqrt_one_minus_na[:, 0:BANK], ALU.mult
+        )
+        nc.scalar.activation(inv_one_minus_na[:, BANK:N], rsqrt_one_minus_na[:, BANK:N], FUNC.Square)
 
         nb_ps = norms.tile([P, BLOCKS], F32, name="nb_ps")
         for i in range(BLOCKS):
@@ -95,16 +101,10 @@ def tile_distance2centroids_kernel(tc, base, pts, cent, offs, out):
 
         y = [held.tile([P, N], F32, name=f"y{i}") for i in range(BLOCKS)]
         y_poly = [held.tile([P, N], F32, name=f"y_poly{i}") for i in range(BLOCKS - 1)]
-        squared_halves = []
         for pair in pairs:
             for i, h in pair:
                 rows = slice(i * P, (i + 1) * P)
                 cols = slice(h * BANK, (h + 1) * BANK)
-                if h not in squared_halves:
-                    squared_halves.append(h)
-                    nc.vector.tensor_tensor(
-                        inv_one_minus_na[:, cols], rsqrt_one_minus_na[:, cols], rsqrt_one_minus_na[:, cols], ALU.mult
-                    )
                 dot_ps = dots.tile([P, BANK], F32, name="dot_ps", tag="dot")
                 for k in range(CHUNKS):
                     nc.tensor.matmul(

@@ -99,8 +99,9 @@ def tile_distance2centroids_kernel(tc, base, pts, cent, offs, out):
         pairs = [[(i, h) for i in range(BLOCKS - 1)] for h in range(HALVES)]
         pairs.append([(BLOCKS - 1, h) for h in range(HALVES)])
 
+        last_piece = pairs[-1][-1]
         y = [held.tile([P, N], F32, name=f"y{i}") for i in range(BLOCKS)]
-        y_poly = [held.tile([P, N], F32, name=f"y_poly{i}") for i in range(BLOCKS - 1)]
+        y_poly = [held.tile([P, N], F32, name=f"y_poly{i}") for i in range(BLOCKS)]
         for pair in pairs:
             for i, h in pair:
                 rows = slice(i * P, (i + 1) * P)
@@ -114,7 +115,7 @@ def tile_distance2centroids_kernel(tc, base, pts, cent, offs, out):
                     out=y[i][:, cols], in0=dot_ps[:], scalar=one_plus_nb[:, i : i + 1],
                     in1=inv_one_minus_na[:, cols], op0=ALU.add, op1=ALU.mult,
                 )
-                if i < BLOCKS - 1:
+                if (i, h) != last_piece:
                     nc.vector.scalar_tensor_tensor(
                         out=y_poly[i][:, cols], in0=y[i][:, cols], scalar=one_plus_nb[:, i : i + 1],
                         in1=y[i][:, cols], op0=ALU.subtract, op1=ALU.mult,
@@ -125,7 +126,7 @@ def tile_distance2centroids_kernel(tc, base, pts, cent, offs, out):
             root = held.tile([P, len(pair), BANK], F32, name="root", tag="root")
             for q, (i, h) in enumerate(pair):
                 cols = slice(h * BANK, (h + 1) * BANK)
-                if i < BLOCKS - 1:
+                if (i, h) != last_piece:
                     nc.scalar.activation(root[:, q, :], y_poly[i][:, cols], FUNC.Sqrt, bias=nb[:, i : i + 1])
                 else:
                     nc.scalar.activation(

@@ -12,8 +12,6 @@ CHUNKS = D // P
 BANK = 512
 HALVES = N // BANK
 
-WARM_UPS = 4
-
 FLOPS = 2 * C * N * D
 
 
@@ -40,9 +38,6 @@ def tile_distance2centroids_kernel(tc, base, pts, cent, offs, out):
 
         ones = held.tile([P, BANK], BF16, name="ones")
         nc.vector.memset(ones[:], 1.0)
-        warm_ps = dots.tile([P, BANK], F32, name="warm_ps", tag="dot")
-        for w in range(WARM_UPS):
-            nc.tensor.matmul(warm_ps[:], ones[:, 0:P], ones[:], start=True, stop=True)
         ident = held.tile([P, P], F32, name="ident")
         make_identity(nc, ident[:])
         cent_sq = held.tile([P, CHUNKS, N], BF16, name="cent_sq")

import concourse.mybir as mybir
from concourse.masks import make_identity

F32, BF16, U16 = mybir.dt.float32, mybir.dt.bfloat16, mybir.dt.uint16
ALU = mybir.AluOpType
FUNC = mybir.ActivationFunctionType

P = 128
C, S, N, D = 384, 4096, 1024, 256
BLOCKS = C // P
CHUNKS = D // P
BANK = 512
HALVES = N // BANK

FLOPS = 2 * C * N * D


def tile_distance2centroids_kernel(tc, base, pts, cent, offs, out):
    nc = tc.nc
    with (
        tc.tile_pool(name="held", bufs=1) as held,
        tc.psum_pool(name="dots", bufs=5) as dots,
        tc.psum_pool(name="sums", bufs=2) as sums,
        tc.psum_pool(name="norms", bufs=1) as norms,
    ):
        cent_sb = held.tile([P, CHUNKS, N], BF16, name="cent_sb")
        for h in range(HALVES):
            cols = slice(h * BANK, (h + 1) * BANK)
            for k in range(CHUNKS):
                nc.sync.dma_start(cent_sb[:, k, cols], cent[k * P : (k + 1) * P, cols])
        pts_sb = held.tile([P, CHUNKS, C], BF16, name="pts_sb")
        nc.sync.dma_start(pts_sb[:], pts.rearrange("(k p) c -> p k c", p=P))
        offsets = held.tile([P, N // 16], U16, name="offsets")
        nc.sync.dma_start(offsets[:], offs)
        windows = [held.tile([P, S], F32, name=f"window{i}") for i in range(BLOCKS)]
        for i in range(BLOCKS):
            nc.sync.dma_start(windows[i][:], base[i * P : (i + 1) * P, :])

        ones = held.tile([P, BANK], BF16, name="ones")
        nc.vector.memset(ones[:], 1.0)
        ident = held.tile([P, P], F32, name="ident")
        make_identity(nc, ident[:])
        cent_sq = held.tile([P, CHUNKS, N], BF16, name="cent_sq")
        for h in range(HALVES):
            cols = slice(h * BANK, (h + 1) * BANK)
            for k in range(CHUNKS):
                nc.vector.tensor_tensor(cent_sq[:, k, cols], cent_sb[:, k, cols], cent_sb[:, k, cols], ALU.mult)
        pts_sq = held.tile([P, CHUNKS, C], BF16, name="pts_sq")
        nc.vector.tensor_tensor(pts_sq[:], pts_sb[:], pts_sb[:], ALU.mult)
        pts_m2 = held.tile([P, CHUNKS, C], BF16, name="pts_m2")
        nc.vector.tensor_scalar(out=pts_m2[:], in0=pts_sb[:], scalar1=-2.0, scalar2=None, op0=ALU.mult)

        rsqrt_one_minus_na = held.tile([P, N], F32, name="rsqrt_one_minus_na")
        inv_one_minus_na = held.tile([P, N], F32, name="inv_one_minus_na")
        for h in range(HALVES):
            cols = slice(h * BANK, (h + 1) * BANK)
            na_ps = dots.tile([P, BANK], F32, name="na_ps", tag="dot")
            for k in range(CHUNKS):
                nc.tensor.matmul(na_ps[:], ones[:, 0:P], cent_sq[:, k, cols], start=(k == 0), stop=(k == CHUNKS - 1))
            nc.scalar.activation(
                rsqrt_one_minus_na[:, cols], na_ps[:], FUNC.Abs_reciprocal_sqrt, bias=1.0, scale=-1.0
            )
        nc.vector.tensor_tensor(
            inv_one_minus_na[:, 0:BANK], rsqrt_one_minus_na[:, 0:BANK], rsqrt_one_minus_na[:, 0:BANK], ALU.mult
        )
        nc.scalar.activation(inv_one_minus_na[:, BANK:N], rsqrt_one_minus_na[:, BANK:N], FUNC.Square)

        nb_ps = norms.tile([P, BLOCKS], F32, name="nb_ps")
        for i in range(BLOCKS):
            for k in range(CHUNKS):
                nc.tensor.matmul(
                    nb_ps[:, i : i + 1], pts_sq[:, k, i * P : (i + 1) * P], ones[:, 0:1],
                    start=(k == 0), stop=(k == CHUNKS - 1),
                )
        nb = held.tile([P, BLOCKS], F32, name="nb")
        nc.vector.tensor_copy(nb[:], nb_ps[:])
        one_plus_nb = held.tile([P, BLOCKS], F32, name="one_plus_nb")
        nc.vector.tensor_scalar(out=one_plus_nb[:], in0=nb_ps[:], scalar1=1.0, scalar2=None, op0=ALU.add)
        minus_half_one_plus_nb = held.tile([P, BLOCKS], F32, name="minus_half_one_plus_nb")
        nc.vector.tensor_scalar(
            out=minus_half_one_plus_nb[:], in0=nb_ps[:], scalar1=-0.5, scalar2=-0.5, op0=ALU.mult, op1=ALU.add
        )
        inv_r = held.tile([P, BLOCKS], F32, name="inv_r")
        nc.vector.tensor_scalar(out=inv_r[:], in0=nb_ps[:], scalar1=-0.5, scalar2=0.5, op0=ALU.mult, op1=ALU.add)
        minus_inv_r_sq = held.tile([P, BLOCKS], F32, name="minus_inv_r_sq")
        nc.vector.scalar_tensor_tensor(
            out=minus_inv_r_sq[:], in0=inv_r[:], scalar=-1.0, in1=inv_r[:], op0=ALU.mult, op1=ALU.mult
        )
        r = held.tile([P, BLOCKS], F32, name="r")
        nc.vector.reciprocal(r[:], inv_r[:])
        one_minus_r = held.tile([P, BLOCKS], F32, name="one_minus_r")
        nc.vector.tensor_scalar(out=one_minus_r[:], in0=r[:], scalar1=-1.0, scalar2=1.0, op0=ALU.mult, op1=ALU.add)

        pairs = [[(i, h) for i in range(BLOCKS - 1)] for h in range(HALVES)]
        pairs.append([(BLOCKS - 1, h) for h in range(HALVES)])

        last_piece = pairs[-1][-1]
        y = [held.tile([P, N], F32, name=f"y{i}") for i in range(BLOCKS)]
        y_poly = [held.tile([P, N], F32, name=f"y_poly{i}") for i in range(BLOCKS)]
        for pair in pairs:
            for i, h in pair:
                rows = slice(i * P, (i + 1) * P)
                cols = slice(h * BANK, (h + 1) * BANK)
                dot_ps = dots.tile([P, BANK], F32, name="dot_ps", tag="dot")
                for k in range(CHUNKS):
                    nc.tensor.matmul(
                        dot_ps[:], pts_m2[:, k, rows], cent_sb[:, k, cols], start=(k == 0), stop=(k == CHUNKS - 1)
                    )
                nc.vector.scalar_tensor_tensor(
                    out=y[i][:, cols], in0=dot_ps[:], scalar=one_plus_nb[:, i : i + 1],
                    in1=inv_one_minus_na[:, cols], op0=ALU.add, op1=ALU.mult,
                )
                if (i, h) != last_piece:
                    nc.vector.scalar_tensor_tensor(
                        out=y_poly[i][:, cols], in0=y[i][:, cols], scalar=one_plus_nb[:, i : i + 1],
                        in1=y[i][:, cols], op0=ALU.subtract, op1=ALU.mult,
                    )

        dist = [held.tile([P, N], F32, name=f"dist{i}") for i in range(BLOCKS)]
        for pair in pairs:
            root = held.tile([P, len(pair), BANK], F32, name="root", tag="root")
            for q, (i, h) in enumerate(pair):
                cols = slice(h * BANK, (h + 1) * BANK)
                if (i, h) != last_piece:
                    nc.scalar.activation(root[:, q, :], y_poly[i][:, cols], FUNC.Sqrt, bias=nb[:, i : i + 1])
                else:
                    nc.scalar.activation(
                        root[:, q, :], y[i][:, cols], FUNC.Square, bias=minus_half_one_plus_nb[:, i : i + 1]
                    )
                    nc.scalar.activation(root[:, q, :], root[:, q, :], FUNC.Sqrt, bias=minus_inv_r_sq[:, i : i + 1])
            for q, (i, h) in enumerate(pair):
                cols = slice(h * BANK, (h + 1) * BANK)
                sum_ps = sums.tile([P, BANK], F32, name="sum_ps", tag="sum")
                nc.tensor.matmul(sum_ps[:], ident[:], y[i][:, cols], start=True, stop=False)
                nc.tensor.matmul(sum_ps[:], ident[:], root[:, q, :], start=False, stop=True)
                nc.scalar.activation(
                    dist[i][:, cols], sum_ps[:], FUNC.Ln, bias=one_minus_r[:, i : i + 1], scale=r[:, i : i + 1]
                )
            for i, h in pair:
                cols = slice(h * BANK, (h + 1) * BANK)
                piece = offsets[:, h * (BANK // 16) : (h + 1) * (BANK // 16)]
                nc.vector.tensor_tensor(windows[i][:].indirect(piece), dist[i][:, cols], dist[i][:, cols], ALU.mult)
                if h == HALVES - 1:
                    nc.sync.dma_start(out[i * P : (i + 1) * P, :], windows[i][:])
